import numpy as np
import ml_dtypes


def mxq(x, axis, fmt="e4m3"):
    dtype, down = {"e4m3": (ml_dtypes.float8_e4m3fn, 7), "e5m2": (ml_dtypes.float8_e5m2, 14)}[fmt]
    v = np.moveaxis(np.asarray(x, np.float32).astype(ml_dtypes.bfloat16).astype(np.float64), axis, -1)
    blocks = v.reshape(v.shape[:-1] + (-1, 32))
    amax = np.abs(blocks).max(-1, keepdims=True)
    byte = np.maximum(np.where(amax > 0, np.frexp(amax)[1] - 1 + 127, 0) - down, 1)
    scale = np.exp2(byte - 127.0)
    codes = (blocks / scale).astype(np.float32).astype(dtype).astype(np.float64)
    return np.moveaxis((codes * scale).reshape(v.shape), -1, axis)


WIDE = False


def mx_kscale(k):
    if not WIDE:
        return np.ones(k)
    levels = np.array([10, -10, 5, -5, 0])
    a = np.random.permutation(np.resize(levels, k // 512 * 4)).reshape(k // 512, 4)
    idx = np.arange(k)
    return np.exp2(a[idx // 512, idx % 128 // 32])


BF16 = ml_dtypes.bfloat16


def bf(x):
    return np.asarray(x, np.float32).astype(BF16)


def f64(x):
    return np.asarray(x).astype(np.float64)


E2M1 = np.array([0.0, 0.5, 1.0, 1.5, 2.0, 3.0, 4.0, 6.0, -0.0, -0.5, -1.0, -1.5, -2.0, -3.0, -4.0, -6.0])


def pack_weight(w, fmt):
    k, n = w.shape
    w = f64(bf(w)).reshape(k // 32, 32, n)
    amax = np.abs(w).max(1)
    if fmt == "e4m3":
        byte = np.frexp(amax)[1] - 1 + 127 - 7
    else:
        mant, ex = np.frexp(amax / 6.0)
        byte = np.where(mant > 0.5, ex, ex - 1) + 127
    byte = np.clip(np.where(amax > 0, byte, 1), 1, 254)
    scaled = (w * np.exp2(127.0 - byte)[:, None, :]).reshape(k, n).astype(np.float32)
    by_word = np.ascontiguousarray(scaled.reshape(k // 512, 128, 4, n).transpose(0, 1, 3, 2))
    if fmt == "e4m3":
        words = by_word.astype(ml_dtypes.float8_e4m3fn).view(np.uint8)
    else:
        c = by_word.astype(ml_dtypes.float4_e2m1fn).view(np.uint8) & 0xF
        words = c[..., 0::2] | (c[..., 1::2] << 4)
    return np.ascontiguousarray(words), np.ascontiguousarray(byte.astype(np.uint8).reshape(k // 512, 16, n))


def unpack_weight(words, scales, fmt):
    g, p, n, _ = words.shape
    if fmt == "e4m3":
        vals = np.ascontiguousarray(words).view(ml_dtypes.float8_e4m3fn).astype(np.float64)
    else:
        nib = np.empty((g, p, n, 4), np.uint8)
        nib[..., 0::2] = words & 0xF
        nib[..., 1::2] = words >> 4
        vals = E2M1[nib]
    vals = vals * np.repeat(np.exp2(scales.astype(np.float64) - 127.0), 8, axis=1)[..., None]
    return vals.transpose(0, 1, 3, 2).reshape(g * 512, n)


B, T, V, C, K, R = 8, 16, 32, 512, 512, 256
FMT = "e4m3"


def setup_inputs():
    n = np.random.standard_normal
    s = mx_kscale(C)
    x = 0.7 * n((B, 1, V, C)) + 0.7 * n((B, T, V, C))
    A = bf(np.eye(V) + 0.1 * n((K, V, V)))
    lam = bf(0.25 + 0.1 * np.random.random(1))
    phi_w_words, phi_w_scales = pack_weight(n((C, K)) / np.sqrt(C) / s[:, None], FMT)
    phi_b = bf(0.3 * n(K))
    theta_w_words, theta_w_scales = pack_weight(n((C, K)) / np.sqrt(C) / s[:, None], FMT)
    theta_b = bf(0.3 * n(K))
    kappa_w_words, kappa_w_scales = pack_weight(n((K, K)) / np.sqrt(K), FMT)
    kappa_b = bf(0.3 * n(K))
    return {
        "x": bf(x * s),
        "A": A,
        "lam": lam,
        "phi_w_words": phi_w_words,
        "phi_w_scales": phi_w_scales,
        "phi_b": phi_b,
        "theta_w_words": theta_w_words,
        "theta_w_scales": theta_w_scales,
        "theta_b": theta_b,
        "kappa_w_words": kappa_w_words,
        "kappa_w_scales": kappa_w_scales,
        "kappa_b": kappa_b,
    }


def reference(x, A, lam, phi_w_words, phi_w_scales, phi_b, theta_w_words, theta_w_scales, theta_b, kappa_w_words, kappa_w_scales, kappa_b):
    xq = mxq(f64(x), 3, "e4m3")
    phi_x = ((xq @ unpack_weight(phi_w_words, phi_w_scales, FMT)) + f64(phi_b)).mean(axis=1)
    theta_x = ((xq @ unpack_weight(theta_w_words, theta_w_scales, FMT)) + f64(theta_b)).mean(axis=1)
    F_ij = np.tanh(phi_x[:, :, None, :] - theta_x[:, None, :, :])
    A_hat = np.transpose((mxq(F_ij, 3, "e4m3") @ unpack_weight(kappa_w_words, kappa_w_scales, FMT)) + f64(kappa_b), (0, 3, 1, 2))
    return f64(A)[None] + f64(lam) * A_hat

@@ -1,0 +1,298 @@
+from contextlib import ExitStack
+
+import concourse.mybir as mybir
+from concourse.masks import make_identity
+
+F32 = mybir.dt.float32
+BF16 = mybir.dt.bfloat16
+I32 = mybir.dt.int32
+U32 = mybir.dt.uint32
+U8 = mybir.dt.uint8
+FP8X4 = mybir.dt.float8_e4m3fn_x4
+ALU = mybir.AluOpType
+ACT = mybir.ActivationFunctionType
+
+BATCH, TIME, JOINTS, CH = 8, 16, 32, 512
+P = 128
+PACK = 4
+T_GROUPS = TIME * JOINTS // P
+K_CHUNKS = CH // P
+U_HALF = JOINTS // 2
+PAIRS = U_HALF * JOINTS
+STEPS = 2 * BATCH
+PHI, THETA, KAPPA = 0, 1, 2
+
+U_GPSIMD = 10
+
+LEAD_QUANTISE_F = 1
+LEAD_TANH = 2
+LEAD_SUBTRACT = 3
+LEAD_MEANS = 4
+LEAD_FIRST_PRODUCTS = 5
+LEAD_QUANTISE_X = 6
+
+FLOPS = 2 * BATCH * TIME * JOINTS * CH * 2 * CH + 2 * BATCH * JOINTS * JOINTS * CH * CH
+
+
+def run_half(stage, half):
+    if 0 <= half < STEPS:
+        stage(half)
+
+
+def run_batch(stage, first_half):
+    if first_half % 2 == 0 and 0 <= first_half < STEPS:
+        stage(first_half // 2)
+
+
+def tile_attgcn_pa_t_kernel(
+    tc,
+    x,
+    A,
+    lam,
+    phi_w_words,
+    phi_w_scales,
+    phi_b,
+    theta_w_words,
+    theta_w_scales,
+    theta_b,
+    kappa_w_words,
+    kappa_w_scales,
+    kappa_b,
+    out,
+):
+    nc = tc.nc
+    with ExitStack() as ctx:
+        ctx.enter_context(tc.manual_schedule())
+        keep = ctx.enter_context(tc.tile_pool(name="keep", bufs=1))
+        ring = ctx.enter_context(tc.tile_pool(name="ring", bufs=2))
+        psum = ctx.enter_context(tc.psum_pool(name="psum", bufs=1))
+
+        planes = keep.tile([P, 3, CH], U8, align_bytes=64)
+        nc.vector.memset(planes[:].bitcast(I32), 0)
+
+        def load_words(words_dram, name):
+            words = keep.tile([P, CH], U32, align_bytes=64, name=name)
+            nc.sync.dma_start(
+                out=words[:].bitcast(I32),
+                in_=words_dram[0].rearrange("p n t -> p (n t)").bitcast(I32),
+            )
+            return words
+
+        def load_scales(scales_dram, which):
+            for quadrant in range(4):
+                nc.sync.dma_start(
+                    out=planes[32 * quadrant : 32 * quadrant + 4, which, :].bitcast(I32),
+                    in_=scales_dram[0, 4 * quadrant : 4 * quadrant + 4, :].bitcast(I32),
+                )
+
+        def load_x(b):
+            x_rows = keep.tile([P, T_GROUPS, CH], BF16, name="x_rows%d" % b)
+            nc.sync.dma_start(
+                out=x_rows[:], in_=x[b].rearrange("(g r) v c -> (r v) g c", g=T_GROUPS)
+            )
+            return x_rows
+
+        x_tiles = [load_x(0)]
+        phi_words = load_words(phi_w_words, "phi_words")
+        theta_words = load_words(theta_w_words, "theta_words")
+        load_scales(phi_w_scales, PHI)
+        load_scales(theta_w_scales, THETA)
+        a_bf = keep.tile([P, K_CHUNKS, JOINTS * JOINTS], BF16)
+        nc.sync.dma_start(out=a_bf[:], in_=A.rearrange("(j k) u v -> k j (u v)", j=K_CHUNKS))
+        x_tiles.append(load_x(1))
+        kappa_words = load_words(kappa_w_words, "kappa_words")
+        load_scales(kappa_w_scales, KAPPA)
+        for b in range(2, BATCH):
+            x_tiles.append(load_x(b))
+
+        ident = keep.tile([P, P], F32)
+        make_identity(nc, ident[:])
+
+        lam_bf = keep.tile([P, 1], BF16)
+        nc.gpsimd.dma_start(out=lam_bf[:], in_=lam.partition_broadcast(P))
+        kappa_b_bf = keep.tile([P, K_CHUNKS], BF16)
+        with nc.allow_non_contiguous_dma(reason="512 bias values, one to a partition and chunk"):
+            nc.gpsimd.dma_start(
+                out=kappa_b_bf[:], in_=kappa_b.rearrange("(j k) -> k j", j=K_CHUNKS)
+            )
+        phi_b_bf = keep.tile([P, PACK], BF16)
+        nc.gpsimd.dma_start(out=phi_b_bf[:], in_=phi_b.rearrange("(q k) -> q k", k=PACK))
+        theta_b_bf = keep.tile([P, PACK], BF16)
+        nc.gpsimd.dma_start(out=theta_b_bf[:], in_=theta_b.rearrange("(q k) -> q k", k=PACK))
+
+        averager = keep.tile([P, JOINTS], F32)
+        nc.vector.tensor_reduce(
+            out=averager[:],
+            in_=ident[:].rearrange("p (r v) -> p v r", v=JOINTS),
+            axis=mybir.AxisListType.X,
+            op=ALU.add,
+        )
+        nc.vector.tensor_scalar_mul(out=averager[:], in0=averager[:], scalar1=1.0 / TIME)
+
+        warm = keep.tile([P, 1], F32)
+        nc.vector.memset(warm[:], 0.0)
+        nc.scalar.activation(out=warm[:], in_=warm[:], func=ACT.Tanh)
+
+        lam_col = keep.tile([P, 1], F32)
+        lam_kappa_b = keep.tile([P, K_CHUNKS], F32)
+        bias = keep.tile([P, 2, PACK], F32)
+        a_plus = keep.tile([P, K_CHUNKS, JOINTS * JOINTS], F32)
+
+        def prepare_small_vectors_and_a():
+            nc.vector.tensor_copy(out=lam_col[:], in_=lam_bf[:])
+            nc.vector.tensor_scalar_mul(
+                out=lam_kappa_b[:], in0=kappa_b_bf[:], scalar1=lam_col[:, 0:1]
+            )
+            nc.vector.tensor_copy(out=bias[:, PHI, :], in_=phi_b_bf[:])
+            nc.vector.tensor_copy(out=bias[:, THETA, :], in_=theta_b_bf[:])
+            for j in range(K_CHUNKS):
+                engine = nc.vector if j % 2 == 0 else nc.gpsimd
+                engine.tensor_scalar(
+                    out=a_plus[:, j, :],
+                    in0=a_bf[:, j, :],
+                    scalar1=1.0,
+                    scalar2=lam_kappa_b[:, j : j + 1],
+                    op0=ALU.mult,
+                    op1=ALU.add,
+                )
+
+        x_codes, x_planes, sums, p_th = {}, {}, {}, {}
+        diffs, f_rounded, f_codes, f_planes = {}, {}, {}, {}
+
+        def quantise_x(b):
+            x_f32 = x_tiles[b][:].bitcast(F32)
+            grouped = ring.tile([P, T_GROUPS * P, PACK], BF16, align_bytes=64)
+            grouped_f32 = grouped[:].rearrange("q r k -> q (r k)").bitcast(F32)
+            grouped_f32 = grouped_f32.rearrange("q (g r w) -> q g r w", g=T_GROUPS, w=2)
+            for first in range(0, T_GROUPS, 2):
+                turned = psum.tile([P, 2, 2, P], F32, bufs=2)
+                for g in range(2):
+                    for w in range(2):
+                        nc.tensor.transpose(
+                            turned[:, g, w, :], x_f32[:, first + g, w : CH // 2 : 2], ident[:]
+                        )
+                nc.scalar.copy(
+                    out=grouped_f32[:, first : first + 2, :, :],
+                    in_=turned[:].rearrange("q g w r -> q g r w"),
+                )
+            codes = ring.tile([P, T_GROUPS * P], U32, align_bytes=64, name="x_codes")
+            plane = ring.tile([P, T_GROUPS * P], U8, align_bytes=64, name="x_plane")
+            nc.vector.quantize_mx(
+                out=codes[:].bitcast(FP8X4),
+                scales=plane[:],
+                in_=grouped[:].rearrange("q r k -> q (r k)"),
+            )
+            x_codes[b], x_planes[b] = codes, plane
+
+        def first_products(b):
+            acc_phi = psum.tile([P, CH], F32)
+            acc_theta = psum.tile([P, CH], F32)
+            for g in range(T_GROUPS):
+                rows = slice(g * P, (g + 1) * P)
+                for acc, words, which in ((acc_phi, phi_words, PHI), (acc_theta, theta_words, THETA)):
+                    nc.tensor.matmul_mx(
+                        out=acc[:],
+                        lhsT=x_codes[b][:, rows].bitcast(FP8X4),
+                        lhsT_scale=x_planes[b][:, rows],
+                        rhs=words[:].bitcast(FP8X4),
+                        rhs_scale=planes[:, which, :],
+                        start=(g == 0),
+                        stop=(g == T_GROUPS - 1),
+                    )
+            partial = ring.tile([P, 2, PACK, P], F32)
+            for acc, which in ((acc_phi, PHI), (acc_theta, THETA)):
+                nc.scalar.copy(
+                    out=partial[:, which, :, :], in_=acc[:].rearrange("r (q k) -> r k q", k=PACK)
+                )
+            sums[b] = partial
+
+        def means(b):
+            mean_ps = psum.tile([P, 2, PACK, JOINTS], F32)
+            for which in (PHI, THETA):
+                for k in range(PACK):
+                    nc.tensor.matmul(
+                        out=mean_ps[:, which, k, :],
+                        lhsT=sums[b][:, which, k, :],
+                        rhs=averager[:],
+                        start=True,
+                        stop=True,
+                    )
+            both = ring.tile([P, 2, JOINTS, PACK], F32)
+            nc.vector.tensor_tensor(
+                out=both[:],
+                in0=mean_ps[:].rearrange("q w k v -> q w v k"),
+                in1=bias[:].unsqueeze(2).to_broadcast([P, 2, JOINTS, PACK]),
+                op=ALU.add,
+            )
+            p_th[b] = both
+
+        def subtract(half):
+            b, u0 = half // 2, (half % 2) * U_HALF
+            shape = [P, U_HALF, JOINTS, PACK]
+            p_all_v = p_th[b][:, PHI, u0 : u0 + U_HALF, :].unsqueeze(2).to_broadcast(shape)
+            th_all_u = p_th[b][:, THETA, :, :].unsqueeze(1).to_broadcast(shape)
+            diff = ring.tile(shape, F32, bufs=3)
+            for engine, us in ((nc.gpsimd, slice(0, U_GPSIMD)), (nc.vector, slice(U_GPSIMD, U_HALF))):
+                engine.tensor_tensor(
+                    out=diff[:, us], in0=p_all_v[:, us], in1=th_all_u[:, us], op=ALU.subtract
+                )
+            diffs[half] = diff
+
+        def tanh(half):
+            rounded = ring.tile([P, PAIRS * PACK], BF16, align_bytes=64, bufs=3)
+            nc.scalar.activation(
+                out=rounded[:], in_=diffs[half][:].rearrange("q u v k -> q (u v k)"), func=ACT.Tanh
+            )
+            f_rounded[half] = rounded
+
+        def quantise_f(half):
+            codes = ring.tile([P, PAIRS], U32, align_bytes=64, bufs=3, name="f_codes")
+            plane = ring.tile([P, PAIRS], U8, align_bytes=64, bufs=3, name="f_plane")
+            nc.vector.quantize_mx(
+                out=codes[:].bitcast(FP8X4), scales=plane[:], in_=f_rounded[half][:]
+            )
+            f_codes[half], f_planes[half] = codes, plane
+
+        def second_product_and_store(half):
+            b = half // 2
+            pairs = slice((half % 2) * PAIRS, (half % 2 + 1) * PAIRS)
+            result = ring.tile([P, K_CHUNKS, PAIRS], F32, bufs=3)
+            for j in range(K_CHUNKS):
+                cols = slice(j * P, (j + 1) * P)
+                g_ps = psum.tile([P, PAIRS], F32, bufs=3)
+                nc.tensor.matmul_mx(
+                    out=g_ps[:],
+                    lhsT=kappa_words[:, cols].bitcast(FP8X4),
+                    lhsT_scale=planes[:, KAPPA, cols],
+                    rhs=f_codes[half][:].bitcast(FP8X4),
+                    rhs_scale=f_planes[half][:],
+                    start=True,
+                    stop=True,
+                )
+                nc.vector.scalar_tensor_tensor(
+                    out=result[:, j, :],
+                    in0=g_ps[:],
+                    scalar=lam_col[:, 0:1],
+                    in1=a_plus[:, j, pairs],
+                    op0=ALU.mult,
+                    op1=ALU.add,
+                )
+            nc.sync.dma_start(
+                out=out[b].rearrange("(j k) u v -> k j (u v)", j=K_CHUNKS)[:, :, pairs],
+                in_=result[:],
+            )
+
+        def step(s):
+            run_half(second_product_and_store, s)
+            run_half(quantise_f, s + LEAD_QUANTISE_F)
+            run_half(tanh, s + LEAD_TANH)
+            run_half(subtract, s + LEAD_SUBTRACT)
+            run_batch(means, s + LEAD_MEANS)
+            run_batch(first_products, s + LEAD_FIRST_PRODUCTS)
+            run_batch(quantise_x, s + LEAD_QUANTISE_X)
+
+        for s in range(-LEAD_QUANTISE_X, -LEAD_MEANS):
+            step(s)
+        prepare_small_vectors_and_a()
+        for s in range(-LEAD_MEANS, STEPS):
+            step(s)

@@ -22,7 +22,7 @@ PAIRS = U_HALF * JOINTS
 STEPS = 2 * BATCH
 PHI, THETA, KAPPA = 0, 1, 2
 
-U_GPSIMD = 10
+U_GPSIMD = 0
 
 LEAD_QUANTISE_F = 1
 LEAD_TANH = 2
@@ -232,10 +232,14 @@ def tile_attgcn_pa_t_kernel(
             p_all_v = p_th[b][:, PHI, u0 : u0 + U_HALF, :].unsqueeze(2).to_broadcast(shape)
             th_all_u = p_th[b][:, THETA, :, :].unsqueeze(1).to_broadcast(shape)
             diff = ring.tile(shape, F32, bufs=3)
-            for engine, us in ((nc.gpsimd, slice(0, U_GPSIMD)), (nc.vector, slice(U_GPSIMD, U_HALF))):
-                engine.tensor_tensor(
-                    out=diff[:, us], in0=p_all_v[:, us], in1=th_all_u[:, us], op=ALU.subtract
-                )
+            for engine, first, last in ((nc.gpsimd, 0, U_GPSIMD), (nc.vector, U_GPSIMD, U_HALF)):
+                if last > first:
+                    engine.tensor_tensor(
+                        out=diff[:, first:last],
+                        in0=p_all_v[:, first:last],
+                        in1=th_all_u[:, first:last],
+                        op=ALU.subtract,
+                    )
             diffs[half] = diff
 
         def tanh(half):

@@ -19,29 +19,22 @@ T_GROUPS = TIME * JOINTS // P
 K_CHUNKS = CH // P
 U_HALF = JOINTS // 2
 PAIRS = U_HALF * JOINTS
-STEPS = 2 * BATCH
+HALVES = 2 * BATCH
 PHI, THETA, KAPPA = 0, 1, 2
 
-U_GPSIMD = 0
+U_GPSIMD = 10
 
 LEAD_QUANTISE_F = 1
 LEAD_TANH = 2
-LEAD_SUBTRACT = 3
+LEAD_SUBTRACT_VECTOR = 2
+LEAD_SUBTRACT_GPSIMD = 3
 LEAD_MEANS = 4
-LEAD_FIRST_PRODUCTS = 5
-LEAD_QUANTISE_X = 6
+LEAD_FIRST_PRODUCT = 5
+LEAD_QUANTISE_X = 7
+LEAD_TURN_X = 8
+LEAD_A = 6
 
 FLOPS = 2 * BATCH * TIME * JOINTS * CH * 2 * CH + 2 * BATCH * JOINTS * JOINTS * CH * CH
-
-
-def run_half(stage, half):
-    if 0 <= half < STEPS:
-        stage(half)
-
-
-def run_batch(stage, first_half):
-    if first_half % 2 == 0 and 0 <= first_half < STEPS:
-        stage(first_half // 2)
 
 
 def tile_attgcn_pa_t_kernel(
@@ -93,13 +86,12 @@ def tile_attgcn_pa_t_kernel(
             return x_rows
 
         x_tiles = [load_x(0)]
-        phi_words = load_words(phi_w_words, "phi_words")
-        theta_words = load_words(theta_w_words, "theta_words")
         load_scales(phi_w_scales, PHI)
         load_scales(theta_w_scales, THETA)
+        weight_words = [load_words(phi_w_words, "phi_words"), load_words(theta_w_words, "theta_words")]
+        x_tiles.append(load_x(1))
         a_bf = keep.tile([P, K_CHUNKS, JOINTS * JOINTS], BF16)
         nc.sync.dma_start(out=a_bf[:], in_=A.rearrange("(j k) u v -> k j (u v)", j=K_CHUNKS))
-        x_tiles.append(load_x(1))
         kappa_words = load_words(kappa_w_words, "kappa_words")
         load_scales(kappa_w_scales, KAPPA)
         for b in range(2, BATCH):
@@ -135,19 +127,21 @@ def tile_attgcn_pa_t_kernel(
 
         lam_col = keep.tile([P, 1], F32)
         lam_kappa_b = keep.tile([P, K_CHUNKS], F32)
-        bias = keep.tile([P, 2, PACK], F32)
+        bias_gap = keep.tile([P, PACK], F32)
         a_plus = keep.tile([P, K_CHUNKS, JOINTS * JOINTS], F32)
 
-        def prepare_small_vectors_and_a():
+        def prepare_small_vectors():
             nc.vector.tensor_copy(out=lam_col[:], in_=lam_bf[:])
             nc.vector.tensor_scalar_mul(
                 out=lam_kappa_b[:], in0=kappa_b_bf[:], scalar1=lam_col[:, 0:1]
             )
-            nc.vector.tensor_copy(out=bias[:, PHI, :], in_=phi_b_bf[:])
-            nc.vector.tensor_copy(out=bias[:, THETA, :], in_=theta_b_bf[:])
-            for j in range(K_CHUNKS):
-                engine = nc.vector if j % 2 == 0 else nc.gpsimd
-                engine.tensor_scalar(
+            nc.vector.tensor_tensor(
+                out=bias_gap[:], in0=theta_b_bf[:], in1=phi_b_bf[:], op=ALU.subtract
+            )
+
+        def add_bias_to_a(j):
+            if j % 2 == 0:
+                nc.gpsimd.tensor_scalar(
                     out=a_plus[:, j, :],
                     in0=a_bf[:, j, :],
                     scalar1=1.0,
@@ -155,92 +149,115 @@ def tile_attgcn_pa_t_kernel(
                     op0=ALU.mult,
                     op1=ALU.add,
                 )
+            else:
+                nc.scalar.activation(
+                    out=a_plus[:, j, :],
+                    in_=a_bf[:, j, :],
+                    func=ACT.Identity,
+                    bias=lam_kappa_b[:, j : j + 1],
+                )
 
-        x_codes, x_planes, sums, p_th = {}, {}, {}, {}
+        grouped_x, x_codes, x_planes, partial_sums, mean_banks, th_shifted = {}, {}, {}, {}, {}, {}
         diffs, f_rounded, f_codes, f_planes = {}, {}, {}, {}
 
-        def quantise_x(b):
+        def turn_x(half):
+            b, first = half // 2, (half % 2) * 2
+            if first == 0:
+                grouped = ring.tile([P, T_GROUPS * P, PACK], BF16, align_bytes=64)
+                grouped_x[b] = grouped
             x_f32 = x_tiles[b][:].bitcast(F32)
-            grouped = ring.tile([P, T_GROUPS * P, PACK], BF16, align_bytes=64)
-            grouped_f32 = grouped[:].rearrange("q r k -> q (r k)").bitcast(F32)
+            grouped_f32 = grouped_x[b][:].rearrange("q r k -> q (r k)").bitcast(F32)
             grouped_f32 = grouped_f32.rearrange("q (g r w) -> q g r w", g=T_GROUPS, w=2)
-            for first in range(0, T_GROUPS, 2):
-                turned = psum.tile([P, 2, 2, P], F32, bufs=2)
-                for g in range(2):
-                    for w in range(2):
-                        nc.tensor.transpose(
-                            turned[:, g, w, :], x_f32[:, first + g, w : CH // 2 : 2], ident[:]
-                        )
-                nc.scalar.copy(
-                    out=grouped_f32[:, first : first + 2, :, :],
-                    in_=turned[:].rearrange("q g w r -> q g r w"),
-                )
-            codes = ring.tile([P, T_GROUPS * P], U32, align_bytes=64, name="x_codes")
-            plane = ring.tile([P, T_GROUPS * P], U8, align_bytes=64, name="x_plane")
-            nc.vector.quantize_mx(
-                out=codes[:].bitcast(FP8X4),
-                scales=plane[:],
-                in_=grouped[:].rearrange("q r k -> q (r k)"),
+            turned = psum.tile([P, 2, 2, P], F32)
+            for g in range(2):
+                for w in range(2):
+                    nc.tensor.transpose(
+                        turned[:, g, w, :], x_f32[:, first + g, w : CH // 2 : 2], ident[:]
+                    )
+            nc.scalar.copy(
+                out=grouped_f32[:, first : first + 2, :, :],
+                in_=turned[:].rearrange("q g w r -> q g r w"),
             )
-            x_codes[b], x_planes[b] = codes, plane
 
-        def first_products(b):
-            acc_phi = psum.tile([P, CH], F32)
-            acc_theta = psum.tile([P, CH], F32)
+        def quantise_x(half):
+            b, rows = half // 2, slice((half % 2) * 2 * P, (half % 2 + 1) * 2 * P)
+            if half % 2 == 0:
+                codes = ring.tile([P, T_GROUPS * P], U32, align_bytes=64, name="x_codes")
+                plane = ring.tile([P, T_GROUPS * P], U8, align_bytes=64, name="x_plane")
+                x_codes[b], x_planes[b] = codes, plane
+            nc.vector.quantize_mx(
+                out=x_codes[b][:, rows].bitcast(FP8X4),
+                scales=x_planes[b][:, rows],
+                in_=grouped_x[b][:, rows, :].rearrange("q r k -> q (r k)"),
+            )
+
+        def first_product(half):
+            b, which = half // 2, half % 2
+            acc = psum.tile([P, CH], F32)
             for g in range(T_GROUPS):
                 rows = slice(g * P, (g + 1) * P)
-                for acc, words, which in ((acc_phi, phi_words, PHI), (acc_theta, theta_words, THETA)):
-                    nc.tensor.matmul_mx(
-                        out=acc[:],
-                        lhsT=x_codes[b][:, rows].bitcast(FP8X4),
-                        lhsT_scale=x_planes[b][:, rows],
-                        rhs=words[:].bitcast(FP8X4),
-                        rhs_scale=planes[:, which, :],
-                        start=(g == 0),
-                        stop=(g == T_GROUPS - 1),
-                    )
-            partial = ring.tile([P, 2, PACK, P], F32)
-            for acc, which in ((acc_phi, PHI), (acc_theta, THETA)):
-                nc.scalar.copy(
-                    out=partial[:, which, :, :], in_=acc[:].rearrange("r (q k) -> r k q", k=PACK)
+                nc.tensor.matmul_mx(
+                    out=acc[:],
+                    lhsT=x_codes[b][:, rows].bitcast(FP8X4),
+                    lhsT_scale=x_planes[b][:, rows],
+                    rhs=weight_words[which][:].bitcast(FP8X4),
+                    rhs_scale=planes[:, which, :],
+                    start=(g == 0),
+                    stop=(g == T_GROUPS - 1),
                 )
-            sums[b] = partial
+            partial = ring.tile([P, PACK, P], F32)
+            nc.scalar.copy(out=partial[:], in_=acc[:].rearrange("r (q k) -> r k q", k=PACK))
+            partial_sums[half] = partial
 
-        def means(b):
-            mean_ps = psum.tile([P, 2, PACK, JOINTS], F32)
-            for which in (PHI, THETA):
-                for k in range(PACK):
-                    nc.tensor.matmul(
-                        out=mean_ps[:, which, k, :],
-                        lhsT=sums[b][:, which, k, :],
-                        rhs=averager[:],
-                        start=True,
-                        stop=True,
-                    )
-            both = ring.tile([P, 2, JOINTS, PACK], F32)
-            nc.vector.tensor_tensor(
-                out=both[:],
-                in0=mean_ps[:].rearrange("q w k v -> q w v k"),
-                in1=bias[:].unsqueeze(2).to_broadcast([P, 2, JOINTS, PACK]),
-                op=ALU.add,
-            )
-            p_th[b] = both
+        def means(half):
+            b, which = half // 2, half % 2
+            if which == PHI:
+                mean_bank = psum.tile([P, 2, PACK, JOINTS], F32, bufs=2)
+                mean_banks[b] = mean_bank
+            for k in range(PACK):
+                nc.tensor.matmul(
+                    out=mean_banks[b][:, which, k, :],
+                    lhsT=partial_sums[half][:, k, :],
+                    rhs=averager[:],
+                    start=True,
+                    stop=True,
+                )
+            if which == THETA:
+                shifted = ring.tile([P, JOINTS, PACK], F32)
+                nc.vector.tensor_tensor(
+                    out=shifted[:],
+                    in0=mean_banks[b][:, THETA, :, :].rearrange("q k v -> q v k"),
+                    in1=bias_gap[:].unsqueeze(1).to_broadcast([P, JOINTS, PACK]),
+                    op=ALU.add,
+                )
+                th_shifted[b] = shifted
 
-        def subtract(half):
-            b, u0 = half // 2, (half % 2) * U_HALF
-            shape = [P, U_HALF, JOINTS, PACK]
-            p_all_v = p_th[b][:, PHI, u0 : u0 + U_HALF, :].unsqueeze(2).to_broadcast(shape)
-            th_all_u = p_th[b][:, THETA, :, :].unsqueeze(1).to_broadcast(shape)
-            diff = ring.tile(shape, F32, bufs=3)
-            for engine, first, last in ((nc.gpsimd, 0, U_GPSIMD), (nc.vector, U_GPSIMD, U_HALF)):
-                if last > first:
-                    engine.tensor_tensor(
-                        out=diff[:, first:last],
-                        in0=p_all_v[:, first:last],
-                        in1=th_all_u[:, first:last],
-                        op=ALU.subtract,
-                    )
+        def mean_p_of(half, first, last):
+            u0 = (half % 2) * U_HALF
+            bank = mean_banks[half // 2]
+            return bank[:, PHI, :, u0 + first : u0 + last].rearrange("q k u -> q u k")
+
+        def subtract_on_gpsimd(half):
+            diff = ring.tile([P, U_HALF, JOINTS, PACK], F32, bufs=3)
             diffs[half] = diff
+            handed = ring.tile([P, U_GPSIMD, PACK], F32)
+            nc.vector.tensor_copy(out=handed[:], in_=mean_p_of(half, 0, U_GPSIMD))
+            shape = [P, U_GPSIMD, JOINTS, PACK]
+            nc.gpsimd.tensor_tensor(
+                out=diff[:, 0:U_GPSIMD],
+                in0=handed[:].unsqueeze(2).to_broadcast(shape),
+                in1=th_shifted[half // 2][:].unsqueeze(1).to_broadcast(shape),
+                op=ALU.subtract,
+            )
+
+        def subtract_on_vector(half):
+            shape = [P, U_HALF - U_GPSIMD, JOINTS, PACK]
+            nc.vector.tensor_tensor(
+                out=diffs[half][:, U_GPSIMD:U_HALF],
+                in0=mean_p_of(half, U_GPSIMD, U_HALF).unsqueeze(2).to_broadcast(shape),
+                in1=th_shifted[half // 2][:].unsqueeze(1).to_broadcast(shape),
+                op=ALU.subtract,
+            )
 
         def tanh(half):
             rounded = ring.tile([P, PAIRS * PACK], BF16, align_bytes=64, bufs=3)
@@ -258,12 +275,12 @@ def tile_attgcn_pa_t_kernel(
             f_codes[half], f_planes[half] = codes, plane
 
         def second_product_and_store(half):
-            b = half // 2
             pairs = slice((half % 2) * PAIRS, (half % 2 + 1) * PAIRS)
+            out_b = out[half // 2].rearrange("(j k) u v -> k j (u v)", j=K_CHUNKS)
             result = ring.tile([P, K_CHUNKS, PAIRS], F32, bufs=3)
             for j in range(K_CHUNKS):
                 cols = slice(j * P, (j + 1) * P)
-                g_ps = psum.tile([P, PAIRS], F32, bufs=3)
+                g_ps = psum.tile([P, PAIRS], F32, bufs=4)
                 nc.tensor.matmul_mx(
                     out=g_ps[:],
                     lhsT=kappa_words[:, cols].bitcast(FP8X4),
@@ -281,22 +298,27 @@ def tile_attgcn_pa_t_kernel(
                     op0=ALU.mult,
                     op1=ALU.add,
                 )
-            nc.sync.dma_start(
-                out=out[b].rearrange("(j k) u v -> k j (u v)", j=K_CHUNKS)[:, :, pairs],
-                in_=result[:],
-            )
+                if j % 2 == 1:
+                    nc.sync.dma_start(out=out_b[:, j - 1 : j + 1, pairs], in_=result[:, j - 1 : j + 1, :])
+
+        def run(stage, index, count):
+            if 0 <= index < count:
+                stage(index)
 
         def step(s):
-            run_half(second_product_and_store, s)
-            run_half(quantise_f, s + LEAD_QUANTISE_F)
-            run_half(tanh, s + LEAD_TANH)
-            run_half(subtract, s + LEAD_SUBTRACT)
-            run_batch(means, s + LEAD_MEANS)
-            run_batch(first_products, s + LEAD_FIRST_PRODUCTS)
-            run_batch(quantise_x, s + LEAD_QUANTISE_X)
+            run(subtract_on_vector, s + LEAD_SUBTRACT_VECTOR, HALVES)
+            run(second_product_and_store, s, HALVES)
+            run(quantise_f, s + LEAD_QUANTISE_F, HALVES)
+            run(quantise_x, s + LEAD_QUANTISE_X, HALVES)
+            run(means, s + LEAD_MEANS, HALVES)
+            run(subtract_on_gpsimd, s + LEAD_SUBTRACT_GPSIMD, HALVES)
+            run(first_product, s + LEAD_FIRST_PRODUCT, HALVES)
+            run(turn_x, s + LEAD_TURN_X, HALVES)
+            run(add_bias_to_a, s + LEAD_A, K_CHUNKS)
+            run(tanh, s + LEAD_TANH, HALVES)
 
-        for s in range(-LEAD_QUANTISE_X, -LEAD_MEANS):
+        for s in range(-LEAD_TURN_X, -LEAD_QUANTISE_X + 1):
             step(s)
-        prepare_small_vectors_and_a()
-        for s in range(-LEAD_MEANS, STEPS):
+        prepare_small_vectors()
+        for s in range(-LEAD_QUANTISE_X + 1, HALVES):
             step(s)

@@ -30,9 +30,10 @@ LEAD_SUBTRACT_VECTOR = 2
 LEAD_SUBTRACT_GPSIMD = 3
 LEAD_MEANS = 4
 LEAD_FIRST_PRODUCT = 5
-LEAD_QUANTISE_X = 7
-LEAD_TURN_X = 8
-LEAD_A = 6
+LEAD_QUANTISE_X = 6
+LEAD_TURN_X = 7
+
+BANK_RING = 6
 
 FLOPS = 2 * BATCH * TIME * JOINTS * CH * 2 * CH + 2 * BATCH * JOINTS * JOINTS * CH * CH
 
@@ -85,21 +86,26 @@ def tile_attgcn_pa_t_kernel(
             )
             return x_rows
 
-        x_tiles = [load_x(0)]
+        x_tiles = [load_x(0), load_x(1)]
         load_scales(phi_w_scales, PHI)
         load_scales(theta_w_scales, THETA)
         weight_words = [load_words(phi_w_words, "phi_words"), load_words(theta_w_words, "theta_words")]
-        x_tiles.append(load_x(1))
+        x_tiles.append(load_x(2))
         a_bf = keep.tile([P, K_CHUNKS, JOINTS * JOINTS], BF16)
         nc.sync.dma_start(out=a_bf[:], in_=A.rearrange("(j k) u v -> k j (u v)", j=K_CHUNKS))
+        x_tiles.append(load_x(3))
         kappa_words = load_words(kappa_w_words, "kappa_words")
         load_scales(kappa_w_scales, KAPPA)
-        for b in range(2, BATCH):
+        for b in range(4, BATCH):
             x_tiles.append(load_x(b))
 
         ident = keep.tile([P, P], F32)
         make_identity(nc, ident[:])
 
+        phi_b_bf = keep.tile([P, PACK], BF16)
+        nc.gpsimd.dma_start(out=phi_b_bf[:], in_=phi_b.rearrange("(q k) -> q k", k=PACK))
+        theta_b_bf = keep.tile([P, PACK], BF16)
+        nc.gpsimd.dma_start(out=theta_b_bf[:], in_=theta_b.rearrange("(q k) -> q k", k=PACK))
         lam_bf = keep.tile([P, 1], BF16)
         nc.gpsimd.dma_start(out=lam_bf[:], in_=lam.partition_broadcast(P))
         kappa_b_bf = keep.tile([P, K_CHUNKS], BF16)
@@ -107,10 +113,6 @@ def tile_attgcn_pa_t_kernel(
             nc.gpsimd.dma_start(
                 out=kappa_b_bf[:], in_=kappa_b.rearrange("(j k) -> k j", j=K_CHUNKS)
             )
-        phi_b_bf = keep.tile([P, PACK], BF16)
-        nc.gpsimd.dma_start(out=phi_b_bf[:], in_=phi_b.rearrange("(q k) -> q k", k=PACK))
-        theta_b_bf = keep.tile([P, PACK], BF16)
-        nc.gpsimd.dma_start(out=theta_b_bf[:], in_=theta_b.rearrange("(q k) -> q k", k=PACK))
 
         averager = keep.tile([P, JOINTS], F32)
         nc.vector.tensor_reduce(
@@ -130,17 +132,15 @@ def tile_attgcn_pa_t_kernel(
         bias_gap = keep.tile([P, PACK], F32)
         a_plus = keep.tile([P, K_CHUNKS, JOINTS * JOINTS], F32)
 
-        def prepare_small_vectors():
+        def prepare_small_vectors_and_a():
+            nc.vector.tensor_tensor(
+                out=bias_gap[:], in0=theta_b_bf[:], in1=phi_b_bf[:], op=ALU.subtract
+            )
             nc.vector.tensor_copy(out=lam_col[:], in_=lam_bf[:])
             nc.vector.tensor_scalar_mul(
                 out=lam_kappa_b[:], in0=kappa_b_bf[:], scalar1=lam_col[:, 0:1]
             )
-            nc.vector.tensor_tensor(
-                out=bias_gap[:], in0=theta_b_bf[:], in1=phi_b_bf[:], op=ALU.subtract
-            )
-
-        def add_bias_to_a(j):
-            if j % 2 == 0:
+            for j in range(K_CHUNKS):
                 nc.gpsimd.tensor_scalar(
                     out=a_plus[:, j, :],
                     in0=a_bf[:, j, :],
@@ -149,51 +149,41 @@ def tile_attgcn_pa_t_kernel(
                     op0=ALU.mult,
                     op1=ALU.add,
                 )
-            else:
-                nc.scalar.activation(
-                    out=a_plus[:, j, :],
-                    in_=a_bf[:, j, :],
-                    func=ACT.Identity,
-                    bias=lam_kappa_b[:, j : j + 1],
-                )
 
         grouped_x, x_codes, x_planes, partial_sums, mean_banks, th_shifted = {}, {}, {}, {}, {}, {}
         diffs, f_rounded, f_codes, f_planes = {}, {}, {}, {}
 
-        def turn_x(half):
-            b, first = half // 2, (half % 2) * 2
-            if first == 0:
-                grouped = ring.tile([P, T_GROUPS * P, PACK], BF16, align_bytes=64)
-                grouped_x[b] = grouped
+        def turn_x(b):
             x_f32 = x_tiles[b][:].bitcast(F32)
-            grouped_f32 = grouped_x[b][:].rearrange("q r k -> q (r k)").bitcast(F32)
+            grouped = ring.tile([P, T_GROUPS * P, PACK], BF16, align_bytes=64)
+            grouped_f32 = grouped[:].rearrange("q r k -> q (r k)").bitcast(F32)
             grouped_f32 = grouped_f32.rearrange("q (g r w) -> q g r w", g=T_GROUPS, w=2)
-            turned = psum.tile([P, 2, 2, P], F32)
-            for g in range(2):
-                for w in range(2):
-                    nc.tensor.transpose(
-                        turned[:, g, w, :], x_f32[:, first + g, w : CH // 2 : 2], ident[:]
-                    )
-            nc.scalar.copy(
-                out=grouped_f32[:, first : first + 2, :, :],
-                in_=turned[:].rearrange("q g w r -> q g r w"),
-            )
+            for first in range(0, T_GROUPS, 2):
+                turned = psum.tile([P, 2, 2, P], F32, tag="bank", bufs=BANK_RING)
+                for g in range(2):
+                    for w in range(2):
+                        nc.tensor.transpose(
+                            turned[:, g, w, :], x_f32[:, first + g, w : CH // 2 : 2], ident[:]
+                        )
+                nc.scalar.copy(
+                    out=grouped_f32[:, first : first + 2, :, :],
+                    in_=turned[:].rearrange("q g w r -> q g r w"),
+                )
+            grouped_x[b] = grouped
 
-        def quantise_x(half):
-            b, rows = half // 2, slice((half % 2) * 2 * P, (half % 2 + 1) * 2 * P)
-            if half % 2 == 0:
-                codes = ring.tile([P, T_GROUPS * P], U32, align_bytes=64, name="x_codes")
-                plane = ring.tile([P, T_GROUPS * P], U8, align_bytes=64, name="x_plane")
-                x_codes[b], x_planes[b] = codes, plane
+        def quantise_x(b):
+            codes = keep.tile([P, T_GROUPS * P], U32, align_bytes=64, name="x_codes%d" % b)
+            plane = keep.tile([P, T_GROUPS * P], U8, align_bytes=64, name="x_plane%d" % b)
             nc.vector.quantize_mx(
-                out=x_codes[b][:, rows].bitcast(FP8X4),
-                scales=x_planes[b][:, rows],
-                in_=grouped_x[b][:, rows, :].rearrange("q r k -> q (r k)"),
+                out=codes[:].bitcast(FP8X4),
+                scales=plane[:],
+                in_=grouped_x[b][:].rearrange("q r k -> q (r k)"),
             )
+            x_codes[b], x_planes[b] = codes, plane
 
         def first_product(half):
             b, which = half // 2, half % 2
-            acc = psum.tile([P, CH], F32)
+            acc = psum.tile([P, CH], F32, tag="bank", bufs=BANK_RING)
             for g in range(T_GROUPS):
                 rows = slice(g * P, (g + 1) * P)
                 nc.tensor.matmul_mx(
@@ -237,24 +227,30 @@ def tile_attgcn_pa_t_kernel(
             bank = mean_banks[half // 2]
             return bank[:, PHI, :, u0 + first : u0 + last].rearrange("q k u -> q u k")
 
+        def gpsimd_share(half):
+            return U_GPSIMD if half >= LEAD_SUBTRACT_VECTOR else 0
+
         def subtract_on_gpsimd(half):
             diff = ring.tile([P, U_HALF, JOINTS, PACK], F32, bufs=3)
             diffs[half] = diff
-            handed = ring.tile([P, U_GPSIMD, PACK], F32)
-            nc.vector.tensor_copy(out=handed[:], in_=mean_p_of(half, 0, U_GPSIMD))
-            shape = [P, U_GPSIMD, JOINTS, PACK]
-            nc.gpsimd.tensor_tensor(
-                out=diff[:, 0:U_GPSIMD],
-                in0=handed[:].unsqueeze(2).to_broadcast(shape),
-                in1=th_shifted[half // 2][:].unsqueeze(1).to_broadcast(shape),
-                op=ALU.subtract,
-            )
+            share = gpsimd_share(half)
+            if share > 0:
+                handed = ring.tile([P, share, PACK], F32)
+                nc.vector.tensor_copy(out=handed[:], in_=mean_p_of(half, 0, share))
+                shape = [P, share, JOINTS, PACK]
+                nc.gpsimd.tensor_tensor(
+                    out=diff[:, 0:share],
+                    in0=handed[:].unsqueeze(2).to_broadcast(shape),
+                    in1=th_shifted[half // 2][:].unsqueeze(1).to_broadcast(shape),
+                    op=ALU.subtract,
+                )
 
         def subtract_on_vector(half):
-            shape = [P, U_HALF - U_GPSIMD, JOINTS, PACK]
+            share = gpsimd_share(half)
+            shape = [P, U_HALF - share, JOINTS, PACK]
             nc.vector.tensor_tensor(
-                out=diffs[half][:, U_GPSIMD:U_HALF],
-                in0=mean_p_of(half, U_GPSIMD, U_HALF).unsqueeze(2).to_broadcast(shape),
+                out=diffs[half][:, share:U_HALF],
+                in0=mean_p_of(half, share, U_HALF).unsqueeze(2).to_broadcast(shape),
                 in1=th_shifted[half // 2][:].unsqueeze(1).to_broadcast(shape),
                 op=ALU.subtract,
             )
@@ -280,7 +276,7 @@ def tile_attgcn_pa_t_kernel(
             result = ring.tile([P, K_CHUNKS, PAIRS], F32, bufs=3)
             for j in range(K_CHUNKS):
                 cols = slice(j * P, (j + 1) * P)
-                g_ps = psum.tile([P, PAIRS], F32, bufs=4)
+                g_ps = psum.tile([P, PAIRS], F32, tag="bank", bufs=BANK_RING)
                 nc.tensor.matmul_mx(
                     out=g_ps[:],
                     lhsT=kappa_words[:, cols].bitcast(FP8X4),
@@ -309,16 +305,16 @@ def tile_attgcn_pa_t_kernel(
             run(subtract_on_vector, s + LEAD_SUBTRACT_VECTOR, HALVES)
             run(second_product_and_store, s, HALVES)
             run(quantise_f, s + LEAD_QUANTISE_F, HALVES)
-            run(quantise_x, s + LEAD_QUANTISE_X, HALVES)
+            run(quantise_x, s + LEAD_QUANTISE_X, BATCH)
             run(means, s + LEAD_MEANS, HALVES)
             run(subtract_on_gpsimd, s + LEAD_SUBTRACT_GPSIMD, HALVES)
             run(first_product, s + LEAD_FIRST_PRODUCT, HALVES)
-            run(turn_x, s + LEAD_TURN_X, HALVES)
-            run(add_bias_to_a, s + LEAD_A, K_CHUNKS)
+            run(turn_x, s + LEAD_TURN_X, BATCH)
             run(tanh, s + LEAD_TANH, HALVES)
 
-        for s in range(-LEAD_TURN_X, -LEAD_QUANTISE_X + 1):
+        first_use = 1 - LEAD_MEANS
+        for s in range(-LEAD_TURN_X, first_use):
             step(s)
-        prepare_small_vectors()
-        for s in range(-LEAD_QUANTISE_X + 1, HALVES):
+        prepare_small_vectors_and_a()
+        for s in range(first_use, HALVES):
             step(s)

@@ -24,13 +24,11 @@ PHI, THETA, KAPPA = 0, 1, 2
 
 U_GPSIMD = 10
 
-LEAD_QUANTISE_F = 1
-LEAD_TANH = 2
-LEAD_SUBTRACT_VECTOR = 2
-LEAD_SUBTRACT_GPSIMD = 3
+LEAD_TANH = 1
+LEAD_SUBTRACT = 2
 LEAD_MEANS = 4
 LEAD_FIRST_PRODUCT = 5
-LEAD_QUANTISE_X = 6
+LEAD_QUANTISE_X = 5
 LEAD_TURN_X = 7
 
 BANK_RING = 6
@@ -80,39 +78,45 @@ def tile_attgcn_pa_t_kernel(
                 )
 
         def load_x(b):
-            x_rows = keep.tile([P, T_GROUPS, CH], BF16, name="x_rows%d" % b)
-            nc.sync.dma_start(
-                out=x_rows[:], in_=x[b].rearrange("(g r) v c -> (r v) g c", g=T_GROUPS)
-            )
-            return x_rows
+            by_group = x[b].rearrange("(g r) v c -> (r v) g c", g=T_GROUPS)
+            tiles = []
+            for pair in range(2):
+                x_rows = keep.tile([P, 2, CH], BF16, name="x_rows%d_%d" % (b, pair))
+                nc.sync.dma_start(out=x_rows[:], in_=by_group[:, 2 * pair : 2 * pair + 2, :])
+                tiles.append(x_rows)
+            return tiles
 
-        x_tiles = [load_x(0), load_x(1)]
+        x_tiles = [load_x(0)]
         load_scales(phi_w_scales, PHI)
         load_scales(theta_w_scales, THETA)
+        x_tiles.append(load_x(1))
         weight_words = [load_words(phi_w_words, "phi_words"), load_words(theta_w_words, "theta_words")]
+        a_by_chunk = A.rearrange("(j k) u v -> j k (u v)", j=K_CHUNKS)
+        a_bf = []
+        for j in range(K_CHUNKS):
+            a_chunk = keep.tile([P, JOINTS * JOINTS], BF16, name="a_bf%d" % j)
+            nc.sync.dma_start(out=a_chunk[:], in_=a_by_chunk[j])
+            a_bf.append(a_chunk)
         x_tiles.append(load_x(2))
-        a_bf = keep.tile([P, K_CHUNKS, JOINTS * JOINTS], BF16)
-        nc.sync.dma_start(out=a_bf[:], in_=A.rearrange("(j k) u v -> k j (u v)", j=K_CHUNKS))
-        x_tiles.append(load_x(3))
-        kappa_words = load_words(kappa_w_words, "kappa_words")
         load_scales(kappa_w_scales, KAPPA)
-        for b in range(4, BATCH):
+        kappa_words = load_words(kappa_w_words, "kappa_words")
+        for b in range(3, BATCH):
             x_tiles.append(load_x(b))
+
+        phi_b_bf = keep.tile([P, PACK], BF16)
+        nc.scalar.dma_start(out=phi_b_bf[:], in_=phi_b.rearrange("(q k) -> q k", k=PACK))
+        theta_b_bf = keep.tile([P, PACK], BF16)
+        nc.scalar.dma_start(out=theta_b_bf[:], in_=theta_b.rearrange("(q k) -> q k", k=PACK))
+        lam_bf = keep.tile([P, 1], BF16)
+        nc.scalar.dma_start(out=lam_bf[:], in_=lam.partition_broadcast(P))
+        kappa_b_bf = keep.tile([P, K_CHUNKS], BF16)
+        with nc.allow_non_contiguous_dma(reason="512 bias values, one to a partition and chunk"):
+            nc.scalar.dma_start(
+                out=kappa_b_bf[:], in_=kappa_b.rearrange("(j k) -> k j", j=K_CHUNKS)
+            )
 
         ident = keep.tile([P, P], F32)
         make_identity(nc, ident[:])
-
-        phi_b_bf = keep.tile([P, PACK], BF16)
-        nc.gpsimd.dma_start(out=phi_b_bf[:], in_=phi_b.rearrange("(q k) -> q k", k=PACK))
-        theta_b_bf = keep.tile([P, PACK], BF16)
-        nc.gpsimd.dma_start(out=theta_b_bf[:], in_=theta_b.rearrange("(q k) -> q k", k=PACK))
-        lam_bf = keep.tile([P, 1], BF16)
-        nc.gpsimd.dma_start(out=lam_bf[:], in_=lam.partition_broadcast(P))
-        kappa_b_bf = keep.tile([P, K_CHUNKS], BF16)
-        with nc.allow_non_contiguous_dma(reason="512 bias values, one to a partition and chunk"):
-            nc.gpsimd.dma_start(
-                out=kappa_b_bf[:], in_=kappa_b.rearrange("(j k) -> k j", j=K_CHUNKS)
-            )
 
         averager = keep.tile([P, JOINTS], F32)
         nc.vector.tensor_reduce(
@@ -130,7 +134,7 @@ def tile_attgcn_pa_t_kernel(
         lam_col = keep.tile([P, 1], F32)
         lam_kappa_b = keep.tile([P, K_CHUNKS], F32)
         bias_gap = keep.tile([P, PACK], F32)
-        a_plus = keep.tile([P, K_CHUNKS, JOINTS * JOINTS], F32)
+        a_plus = []
 
         def prepare_small_vectors_and_a():
             nc.vector.tensor_tensor(
@@ -141,35 +145,37 @@ def tile_attgcn_pa_t_kernel(
                 out=lam_kappa_b[:], in0=kappa_b_bf[:], scalar1=lam_col[:, 0:1]
             )
             for j in range(K_CHUNKS):
-                nc.gpsimd.tensor_scalar(
-                    out=a_plus[:, j, :],
-                    in0=a_bf[:, j, :],
-                    scalar1=1.0,
-                    scalar2=lam_kappa_b[:, j : j + 1],
-                    op0=ALU.mult,
-                    op1=ALU.add,
+                a_chunk = keep.tile([P, JOINTS * JOINTS], F32, name="a_plus%d" % j)
+                nc.vector.tensor_scalar_add(
+                    out=a_chunk[:], in0=a_bf[j][:], scalar1=lam_kappa_b[:, j : j + 1]
                 )
+                a_plus.append(a_chunk)
 
         grouped_x, x_codes, x_planes, partial_sums, mean_banks, th_shifted = {}, {}, {}, {}, {}, {}
         diffs, f_rounded, f_codes, f_planes = {}, {}, {}, {}
 
-        def turn_x(b):
-            x_f32 = x_tiles[b][:].bitcast(F32)
-            grouped = ring.tile([P, T_GROUPS * P, PACK], BF16, align_bytes=64)
-            grouped_f32 = grouped[:].rearrange("q r k -> q (r k)").bitcast(F32)
+        def out_of_psum(engine, dst, src):
+            if engine == "vector":
+                nc.vector.tensor_copy(out=dst, in_=src)
+            else:
+                nc.scalar.copy(out=dst, in_=src)
+
+        def turn_x(b, pair, engine="scalar"):
+            if pair == 0:
+                grouped = ring.tile([P, T_GROUPS * P, PACK], BF16, align_bytes=64, name="grouped")
+                grouped_x[b] = grouped
+            x_f32 = x_tiles[b][pair][:].bitcast(F32)
+            grouped_f32 = grouped_x[b][:].rearrange("q r k -> q (r k)").bitcast(F32)
             grouped_f32 = grouped_f32.rearrange("q (g r w) -> q g r w", g=T_GROUPS, w=2)
-            for first in range(0, T_GROUPS, 2):
-                turned = psum.tile([P, 2, 2, P], F32, tag="bank", bufs=BANK_RING)
-                for g in range(2):
-                    for w in range(2):
-                        nc.tensor.transpose(
-                            turned[:, g, w, :], x_f32[:, first + g, w : CH // 2 : 2], ident[:]
-                        )
-                nc.scalar.copy(
-                    out=grouped_f32[:, first : first + 2, :, :],
-                    in_=turned[:].rearrange("q g w r -> q g r w"),
-                )
-            grouped_x[b] = grouped
+            turned = psum.tile([P, 2, 2, P], F32, tag="bank", bufs=BANK_RING)
+            for g in range(2):
+                for w in range(2):
+                    nc.tensor.transpose(turned[:, g, w, :], x_f32[:, g, w : CH // 2 : 2], ident[:])
+            out_of_psum(
+                engine,
+                grouped_f32[:, 2 * pair : 2 * pair + 2, :, :],
+                turned[:].rearrange("q g w r -> q g r w"),
+            )
 
         def quantise_x(b):
             codes = keep.tile([P, T_GROUPS * P], U32, align_bytes=64, name="x_codes%d" % b)
@@ -181,7 +187,7 @@ def tile_attgcn_pa_t_kernel(
             )
             x_codes[b], x_planes[b] = codes, plane
 
-        def first_product(half):
+        def first_product(half, engine="scalar"):
             b, which = half // 2, half % 2
             acc = psum.tile([P, CH], F32, tag="bank", bufs=BANK_RING)
             for g in range(T_GROUPS):
@@ -195,14 +201,14 @@ def tile_attgcn_pa_t_kernel(
                     start=(g == 0),
                     stop=(g == T_GROUPS - 1),
                 )
-            partial = ring.tile([P, PACK, P], F32)
-            nc.scalar.copy(out=partial[:], in_=acc[:].rearrange("r (q k) -> r k q", k=PACK))
+            partial = ring.tile([P, PACK, P], F32, name="partial")
+            out_of_psum(engine, partial[:], acc[:].rearrange("r (q k) -> r k q", k=PACK))
             partial_sums[half] = partial
 
         def means(half):
             b, which = half // 2, half % 2
             if which == PHI:
-                mean_bank = psum.tile([P, 2, PACK, JOINTS], F32, bufs=2)
+                mean_bank = psum.tile([P, 2, PACK, JOINTS], F32, bufs=2, name="mean_bank")
                 mean_banks[b] = mean_bank
             for k in range(PACK):
                 nc.tensor.matmul(
@@ -212,15 +218,16 @@ def tile_attgcn_pa_t_kernel(
                     start=True,
                     stop=True,
                 )
-            if which == THETA:
-                shifted = ring.tile([P, JOINTS, PACK], F32)
-                nc.vector.tensor_tensor(
-                    out=shifted[:],
-                    in0=mean_banks[b][:, THETA, :, :].rearrange("q k v -> q v k"),
-                    in1=bias_gap[:].unsqueeze(1).to_broadcast([P, JOINTS, PACK]),
-                    op=ALU.add,
-                )
-                th_shifted[b] = shifted
+
+        def shift_mean_th(b):
+            shifted = ring.tile([P, JOINTS, PACK], F32, name="shifted")
+            nc.vector.tensor_tensor(
+                out=shifted[:],
+                in0=mean_banks[b][:, THETA, :, :].rearrange("q k v -> q v k"),
+                in1=bias_gap[:].unsqueeze(1).to_broadcast([P, JOINTS, PACK]),
+                op=ALU.add,
+            )
+            th_shifted[b] = shifted
 
         def mean_p_of(half, first, last):
             u0 = (half % 2) * U_HALF
@@ -228,14 +235,14 @@ def tile_attgcn_pa_t_kernel(
             return bank[:, PHI, :, u0 + first : u0 + last].rearrange("q k u -> q u k")
 
         def gpsimd_share(half):
-            return U_GPSIMD if half >= LEAD_SUBTRACT_VECTOR else 0
+            return U_GPSIMD if half >= 2 else 0
 
         def subtract_on_gpsimd(half):
-            diff = ring.tile([P, U_HALF, JOINTS, PACK], F32, bufs=3)
+            diff = ring.tile([P, U_HALF, JOINTS, PACK], F32, bufs=3, name="diff")
             diffs[half] = diff
             share = gpsimd_share(half)
             if share > 0:
-                handed = ring.tile([P, share, PACK], F32)
+                handed = ring.tile([P, share, PACK], F32, name="handed")
                 nc.vector.tensor_copy(out=handed[:], in_=mean_p_of(half, 0, share))
                 shape = [P, share, JOINTS, PACK]
                 nc.gpsimd.tensor_tensor(
@@ -256,7 +263,7 @@ def tile_attgcn_pa_t_kernel(
             )
 
         def tanh(half):
-            rounded = ring.tile([P, PAIRS * PACK], BF16, align_bytes=64, bufs=3)
+            rounded = ring.tile([P, PAIRS * PACK], BF16, align_bytes=64, bufs=3, name="rounded")
             nc.scalar.activation(
                 out=rounded[:], in_=diffs[half][:].rearrange("q u v k -> q (u v k)"), func=ACT.Tanh
             )
@@ -270,10 +277,8 @@ def tile_attgcn_pa_t_kernel(
             )
             f_codes[half], f_planes[half] = codes, plane
 
-        def second_product_and_store(half):
-            pairs = slice((half % 2) * PAIRS, (half % 2 + 1) * PAIRS)
-            out_b = out[half // 2].rearrange("(j k) u v -> k j (u v)", j=K_CHUNKS)
-            result = ring.tile([P, K_CHUNKS, PAIRS], F32, bufs=3)
+        def second_product(half):
+            banks = []
             for j in range(K_CHUNKS):
                 cols = slice(j * P, (j + 1) * P)
                 g_ps = psum.tile([P, PAIRS], F32, tag="bank", bufs=BANK_RING)
@@ -286,35 +291,73 @@ def tile_attgcn_pa_t_kernel(
                     start=True,
                     stop=True,
                 )
+                banks.append(g_ps)
+            return banks
+
+        def finish_and_store(half, banks):
+            pairs = slice((half % 2) * PAIRS, (half % 2 + 1) * PAIRS)
+            out_b = out[half // 2].rearrange("(j k) u v -> k j (u v)", j=K_CHUNKS)
+            result = ring.tile([P, K_CHUNKS, PAIRS], F32, bufs=3, name="result")
+            for j in range(K_CHUNKS):
                 nc.vector.scalar_tensor_tensor(
                     out=result[:, j, :],
-                    in0=g_ps[:],
+                    in0=banks[j][:],
                     scalar=lam_col[:, 0:1],
-                    in1=a_plus[:, j, pairs],
+                    in1=a_plus[j][:, pairs],
                     op0=ALU.mult,
                     op1=ALU.add,
                 )
                 if j % 2 == 1:
                     nc.sync.dma_start(out=out_b[:, j - 1 : j + 1, pairs], in_=result[:, j - 1 : j + 1, :])
 
-        def run(stage, index, count):
-            if 0 <= index < count:
-                stage(index)
+        turn_x(0, 0)
+        turn_x(0, 1, "vector")
+        quantise_x(0)
+        turn_x(1, 0)
+        turn_x(1, 1)
+        first_product(0)
+        first_product(1)
+        quantise_x(1)
+        prepare_small_vectors_and_a()
+        means(0)
+        means(1)
+        shift_mean_th(0)
+        turn_x(2, 0)
+        turn_x(2, 1)
+        first_product(2)
+        subtract_on_gpsimd(0)
+        subtract_on_vector(0)
+        tanh(0)
+        quantise_x(2)
+        first_product(3, "vector")
+        subtract_on_gpsimd(1)
+        subtract_on_vector(1)
+        means(2)
+        means(3)
+        shift_mean_th(1)
+        first_product(4)
+        turn_x(3, 0)
 
         def step(s):
-            run(subtract_on_vector, s + LEAD_SUBTRACT_VECTOR, HALVES)
-            run(second_product_and_store, s, HALVES)
-            run(quantise_f, s + LEAD_QUANTISE_F, HALVES)
-            run(quantise_x, s + LEAD_QUANTISE_X, BATCH)
-            run(means, s + LEAD_MEANS, HALVES)
-            run(subtract_on_gpsimd, s + LEAD_SUBTRACT_GPSIMD, HALVES)
-            run(first_product, s + LEAD_FIRST_PRODUCT, HALVES)
-            run(turn_x, s + LEAD_TURN_X, BATCH)
-            run(tanh, s + LEAD_TANH, HALVES)
+            if (s + LEAD_QUANTISE_X) % 2 == 0 and (s + LEAD_QUANTISE_X) // 2 < BATCH:
+                quantise_x((s + LEAD_QUANTISE_X) // 2)
+            quantise_f(s)
+            if s + LEAD_SUBTRACT < HALVES:
+                subtract_on_gpsimd(s + LEAD_SUBTRACT)
+            banks = second_product(s)
+            if s + LEAD_SUBTRACT < HALVES:
+                subtract_on_vector(s + LEAD_SUBTRACT)
+            if s + LEAD_TANH < HALVES:
+                tanh(s + LEAD_TANH)
+            if s + LEAD_TURN_X < HALVES:
+                turn_x((s + LEAD_TURN_X) // 2, (s + LEAD_TURN_X) % 2)
+            if s + LEAD_MEANS < HALVES:
+                means(s + LEAD_MEANS)
+            if s + LEAD_FIRST_PRODUCT < HALVES:
+                first_product(s + LEAD_FIRST_PRODUCT)
+            finish_and_store(s, banks)
+            if s + LEAD_MEANS < HALVES and (s + LEAD_MEANS) % 2 == THETA:
+                shift_mean_th((s + LEAD_MEANS) // 2)
 
-        first_use = 1 - LEAD_MEANS
-        for s in range(-LEAD_TURN_X, first_use):
-            step(s)
-        prepare_small_vectors_and_a()
-        for s in range(first_use, HALVES):
+        for s in range(HALVES):
             step(s)

@@ -33,6 +33,8 @@ LEAD_TURN_X = 7
 
 BANK_RING = 6
 
+PLACE_BYTES = U_GPSIMD * JOINTS * PACK * 4
+
 FLOPS = 2 * BATCH * TIME * JOINTS * CH * 2 * CH + 2 * BATCH * JOINTS * JOINTS * CH * CH
 
 
@@ -57,6 +59,7 @@ def tile_attgcn_pa_t_kernel(
         ctx.enter_context(tc.manual_schedule())
         keep = ctx.enter_context(tc.tile_pool(name="keep", bufs=1))
         ring = ctx.enter_context(tc.tile_pool(name="ring", bufs=2))
+        shared = ctx.enter_context(tc.tile_pool(name="shared", bufs=1))
         psum = ctx.enter_context(tc.psum_pool(name="psum", bufs=1))
 
         planes = keep.tile([P, 3, CH], U8, align_bytes=64)
@@ -152,7 +155,8 @@ def tile_attgcn_pa_t_kernel(
                 a_plus.append(a_chunk)
 
         grouped_x, x_codes, x_planes, partial_sums, mean_banks, th_shifted = {}, {}, {}, {}, {}, {}
-        diffs, f_rounded, f_codes, f_planes = {}, {}, {}, {}
+        diffs_gpsimd, diffs_vector, f_rounded, f_codes, f_planes, mean_p_copies = {}, {}, {}, {}, {}, {}
+        g_banks = {}
 
         def out_of_psum(engine, dst, src):
             if engine == "vector":
@@ -229,6 +233,11 @@ def tile_attgcn_pa_t_kernel(
             )
             th_shifted[b] = shifted
 
+        def copy_mean_p(b):
+            p_copy = ring.tile([P, JOINTS, PACK], F32, name="p_copy")
+            nc.scalar.copy(out=p_copy[:], in_=mean_banks[b][:, PHI, :, :].rearrange("q k u -> q u k"))
+            mean_p_copies[b] = p_copy
+
         def mean_p_of(half, first, last):
             u0 = (half % 2) * U_HALF
             bank = mean_banks[half // 2]
@@ -237,17 +246,22 @@ def tile_attgcn_pa_t_kernel(
         def gpsimd_share(half):
             return U_GPSIMD if half >= 2 else 0
 
+        def place(half):
+            return (half % 3) * PLACE_BYTES
+
         def subtract_on_gpsimd(half):
-            diff = ring.tile([P, U_HALF, JOINTS, PACK], F32, bufs=3, name="diff")
-            diffs[half] = diff
             share = gpsimd_share(half)
             if share > 0:
-                handed = ring.tile([P, share, PACK], F32, name="handed")
-                nc.vector.tensor_copy(out=handed[:], in_=mean_p_of(half, 0, share))
+                diff = shared.tile(
+                    [P, share, JOINTS, PACK], F32, offset=place(half), align_bytes=64,
+                    name="diff_gpsimd%d" % (half % 3),
+                )
+                diffs_gpsimd[half] = diff
+                u0 = (half % 2) * U_HALF
                 shape = [P, share, JOINTS, PACK]
                 nc.gpsimd.tensor_tensor(
-                    out=diff[:, 0:share],
-                    in0=handed[:].unsqueeze(2).to_broadcast(shape),
+                    out=diff[:],
+                    in0=mean_p_copies[half // 2][:, u0 : u0 + share, :].unsqueeze(2).to_broadcast(shape),
                     in1=th_shifted[half // 2][:].unsqueeze(1).to_broadcast(shape),
                     op=ALU.subtract,
                 )
@@ -255,17 +269,32 @@ def tile_attgcn_pa_t_kernel(
         def subtract_on_vector(half):
             share = gpsimd_share(half)
             shape = [P, U_HALF - share, JOINTS, PACK]
+            diff = ring.tile(shape, F32, bufs=3, name="diff_vector")
+            diffs_vector[half] = diff
             nc.vector.tensor_tensor(
-                out=diffs[half][:, share:U_HALF],
+                out=diff[:],
                 in0=mean_p_of(half, share, U_HALF).unsqueeze(2).to_broadcast(shape),
                 in1=th_shifted[half // 2][:].unsqueeze(1).to_broadcast(shape),
                 op=ALU.subtract,
             )
 
         def tanh(half):
-            rounded = ring.tile([P, PAIRS * PACK], BF16, align_bytes=64, bufs=3, name="rounded")
+            share = gpsimd_share(half)
+            rounded = shared.tile(
+                [P, PAIRS * PACK], BF16, offset=place(half + 2), align_bytes=64,
+                name="rounded%d" % (half % 3),
+            )
+            split = share * JOINTS * PACK
+            if share > 0:
+                nc.scalar.activation(
+                    out=rounded[:, 0:split],
+                    in_=diffs_gpsimd[half][:].rearrange("q u v k -> q (u v k)"),
+                    func=ACT.Tanh,
+                )
             nc.scalar.activation(
-                out=rounded[:], in_=diffs[half][:].rearrange("q u v k -> q (u v k)"), func=ACT.Tanh
+                out=rounded[:, split : PAIRS * PACK],
+                in_=diffs_vector[half][:].rearrange("q u v k -> q (u v k)"),
+                func=ACT.Tanh,
             )
             f_rounded[half] = rounded
 
@@ -277,9 +306,8 @@ def tile_attgcn_pa_t_kernel(
             )
             f_codes[half], f_planes[half] = codes, plane
 
-        def second_product(half):
-            banks = []
-            for j in range(K_CHUNKS):
+        def second_product(half, pair):
+            for j in (2 * pair, 2 * pair + 1):
                 cols = slice(j * P, (j + 1) * P)
                 g_ps = psum.tile([P, PAIRS], F32, tag="bank", bufs=BANK_RING)
                 nc.tensor.matmul_mx(
@@ -291,24 +319,23 @@ def tile_attgcn_pa_t_kernel(
                     start=True,
                     stop=True,
                 )
-                banks.append(g_ps)
-            return banks
+                g_banks[(half, j)] = g_ps
 
-        def finish_and_store(half, banks):
+        def finish_and_store(half, pair):
             pairs = slice((half % 2) * PAIRS, (half % 2 + 1) * PAIRS)
             out_b = out[half // 2].rearrange("(j k) u v -> k j (u v)", j=K_CHUNKS)
-            result = ring.tile([P, K_CHUNKS, PAIRS], F32, bufs=3, name="result")
-            for j in range(K_CHUNKS):
+            result = ring.tile([P, 2, PAIRS], F32, bufs=6, name="result")
+            for i in range(2):
+                j = 2 * pair + i
                 nc.vector.scalar_tensor_tensor(
-                    out=result[:, j, :],
-                    in0=banks[j][:],
+                    out=result[:, i, :],
+                    in0=g_banks[(half, j)][:],
                     scalar=lam_col[:, 0:1],
                     in1=a_plus[j][:, pairs],
                     op0=ALU.mult,
                     op1=ALU.add,
                 )
-                if j % 2 == 1:
-                    nc.sync.dma_start(out=out_b[:, j - 1 : j + 1, pairs], in_=result[:, j - 1 : j + 1, :])
+            nc.sync.dma_start(out=out_b[:, 2 * pair : 2 * pair + 2, pairs], in_=result[:])
 
         turn_x(0, 0)
         turn_x(0, 1, "vector")
@@ -335,6 +362,7 @@ def tile_attgcn_pa_t_kernel(
         means(2)
         means(3)
         shift_mean_th(1)
+        copy_mean_p(1)
         first_product(4)
         turn_x(3, 0)
 
@@ -344,20 +372,26 @@ def tile_attgcn_pa_t_kernel(
             quantise_f(s)
             if s + LEAD_SUBTRACT < HALVES:
                 subtract_on_gpsimd(s + LEAD_SUBTRACT)
-            banks = second_product(s)
+            second_product(s, 0)
             if s + LEAD_SUBTRACT < HALVES:
                 subtract_on_vector(s + LEAD_SUBTRACT)
             if s + LEAD_TANH < HALVES:
                 tanh(s + LEAD_TANH)
+            if s > 0:
+                finish_and_store(s - 1, 1)
             if s + LEAD_TURN_X < HALVES:
                 turn_x((s + LEAD_TURN_X) // 2, (s + LEAD_TURN_X) % 2)
             if s + LEAD_MEANS < HALVES:
                 means(s + LEAD_MEANS)
+                if (s + LEAD_MEANS) % 2 == THETA:
+                    copy_mean_p((s + LEAD_MEANS) // 2)
             if s + LEAD_FIRST_PRODUCT < HALVES:
                 first_product(s + LEAD_FIRST_PRODUCT)
-            finish_and_store(s, banks)
+            second_product(s, 1)
+            finish_and_store(s, 0)
             if s + LEAD_MEANS < HALVES and (s + LEAD_MEANS) % 2 == THETA:
                 shift_mean_th((s + LEAD_MEANS) // 2)
 
         for s in range(HALVES):
             step(s)
+        finish_and_store(HALVES - 1, 1)

@@ -367,6 +367,8 @@ def tile_attgcn_pa_t_kernel(
         turn_x(3, 0)
 
         def step(s):
+            if s + LEAD_TURN_X < HALVES:
+                turn_x((s + LEAD_TURN_X) // 2, (s + LEAD_TURN_X) % 2)
             if (s + LEAD_QUANTISE_X) % 2 == 0 and (s + LEAD_QUANTISE_X) // 2 < BATCH:
                 quantise_x((s + LEAD_QUANTISE_X) // 2)
             quantise_f(s)
@@ -379,8 +381,6 @@ def tile_attgcn_pa_t_kernel(
                 tanh(s + LEAD_TANH)
             if s > 0:
                 finish_and_store(s - 1, 1)
-            if s + LEAD_TURN_X < HALVES:
-                turn_x((s + LEAD_TURN_X) // 2, (s + LEAD_TURN_X) % 2)
             if s + LEAD_MEANS < HALVES:
                 means(s + LEAD_MEANS)
                 if (s + LEAD_MEANS) % 2 == THETA:

@@ -80,20 +80,21 @@ def tile_attgcn_pa_t_kernel(
                     in_=scales_dram[0, 4 * quadrant : 4 * quadrant + 4, :].bitcast(I32),
                 )
 
-        def load_x(b):
+        def load_x(b, pieces=1):
             by_group = x[b].rearrange("(g r) v c -> (r v) g c", g=T_GROUPS)
-            tiles = []
-            for pair in range(2):
-                x_rows = keep.tile([P, 2, CH], BF16, name="x_rows%d_%d" % (b, pair))
-                nc.sync.dma_start(out=x_rows[:], in_=by_group[:, 2 * pair : 2 * pair + 2, :])
-                tiles.append(x_rows)
-            return tiles
+            x_rows = keep.tile([P, T_GROUPS, CH], BF16, name="x_rows%d" % b)
+            groups = T_GROUPS // pieces
+            for i in range(pieces):
+                part = slice(i * groups, (i + 1) * groups)
+                nc.sync.dma_start(out=x_rows[:, part, :], in_=by_group[:, part, :])
+            return x_rows
 
-        x_tiles = [load_x(0)]
+        x_tiles = [load_x(0, 2)]
         load_scales(phi_w_scales, PHI)
-        load_scales(theta_w_scales, THETA)
+        weight_words = [load_words(phi_w_words, "phi_words")]
         x_tiles.append(load_x(1))
-        weight_words = [load_words(phi_w_words, "phi_words"), load_words(theta_w_words, "theta_words")]
+        load_scales(theta_w_scales, THETA)
+        weight_words.append(load_words(theta_w_words, "theta_words"))
         a_by_chunk = A.rearrange("(j k) u v -> j k (u v)", j=K_CHUNKS)
         a_bf = []
         for j in range(K_CHUNKS):
@@ -106,20 +107,20 @@ def tile_attgcn_pa_t_kernel(
         for b in range(3, BATCH):
             x_tiles.append(load_x(b))
 
-        phi_b_bf = keep.tile([P, PACK], BF16)
-        nc.scalar.dma_start(out=phi_b_bf[:], in_=phi_b.rearrange("(q k) -> q k", k=PACK))
-        theta_b_bf = keep.tile([P, PACK], BF16)
-        nc.scalar.dma_start(out=theta_b_bf[:], in_=theta_b.rearrange("(q k) -> q k", k=PACK))
-        lam_bf = keep.tile([P, 1], BF16)
-        nc.scalar.dma_start(out=lam_bf[:], in_=lam.partition_broadcast(P))
-        kappa_b_bf = keep.tile([P, K_CHUNKS], BF16)
-        with nc.allow_non_contiguous_dma(reason="512 bias values, one to a partition and chunk"):
-            nc.scalar.dma_start(
-                out=kappa_b_bf[:], in_=kappa_b.rearrange("(j k) -> k j", j=K_CHUNKS)
-            )
-
         ident = keep.tile([P, P], F32)
         make_identity(nc, ident[:])
+
+        lam_bf = keep.tile([P, 1], BF16)
+        nc.gpsimd.dma_start(out=lam_bf[:], in_=lam.partition_broadcast(P))
+        kappa_b_bf = keep.tile([P, K_CHUNKS], BF16)
+        with nc.allow_non_contiguous_dma(reason="512 bias values, one to a partition and chunk"):
+            nc.gpsimd.dma_start(
+                out=kappa_b_bf[:], in_=kappa_b.rearrange("(j k) -> k j", j=K_CHUNKS)
+            )
+        phi_b_bf = keep.tile([P, PACK], BF16)
+        nc.gpsimd.dma_start(out=phi_b_bf[:], in_=phi_b.rearrange("(q k) -> q k", k=PACK))
+        theta_b_bf = keep.tile([P, PACK], BF16)
+        nc.gpsimd.dma_start(out=theta_b_bf[:], in_=theta_b.rearrange("(q k) -> q k", k=PACK))
 
         averager = keep.tile([P, JOINTS], F32)
         nc.vector.tensor_reduce(
@@ -140,9 +141,6 @@ def tile_attgcn_pa_t_kernel(
         a_plus = []
 
         def prepare_small_vectors_and_a():
-            nc.vector.tensor_tensor(
-                out=bias_gap[:], in0=theta_b_bf[:], in1=phi_b_bf[:], op=ALU.subtract
-            )
             nc.vector.tensor_copy(out=lam_col[:], in_=lam_bf[:])
             nc.vector.tensor_scalar_mul(
                 out=lam_kappa_b[:], in0=kappa_b_bf[:], scalar1=lam_col[:, 0:1]
@@ -153,6 +151,9 @@ def tile_attgcn_pa_t_kernel(
                     out=a_chunk[:], in0=a_bf[j][:], scalar1=lam_kappa_b[:, j : j + 1]
                 )
                 a_plus.append(a_chunk)
+            nc.vector.tensor_tensor(
+                out=bias_gap[:], in0=theta_b_bf[:], in1=phi_b_bf[:], op=ALU.subtract
+            )
 
         grouped_x, x_codes, x_planes, partial_sums, mean_banks, th_shifted = {}, {}, {}, {}, {}, {}
         diffs_gpsimd, diffs_vector, f_rounded, f_codes, f_planes, mean_p_copies = {}, {}, {}, {}, {}, {}
@@ -168,13 +169,15 @@ def tile_attgcn_pa_t_kernel(
             if pair == 0:
                 grouped = ring.tile([P, T_GROUPS * P, PACK], BF16, align_bytes=64, name="grouped")
                 grouped_x[b] = grouped
-            x_f32 = x_tiles[b][pair][:].bitcast(F32)
+            x_f32 = x_tiles[b][:].bitcast(F32)
             grouped_f32 = grouped_x[b][:].rearrange("q r k -> q (r k)").bitcast(F32)
             grouped_f32 = grouped_f32.rearrange("q (g r w) -> q g r w", g=T_GROUPS, w=2)
             turned = psum.tile([P, 2, 2, P], F32, tag="bank", bufs=BANK_RING)
             for g in range(2):
                 for w in range(2):
-                    nc.tensor.transpose(turned[:, g, w, :], x_f32[:, g, w : CH // 2 : 2], ident[:])
+                    nc.tensor.transpose(
+                        turned[:, g, w, :], x_f32[:, 2 * pair + g, w : CH // 2 : 2], ident[:]
+                    )
             out_of_psum(
                 engine,
                 grouped_f32[:, 2 * pair : 2 * pair + 2, :, :],

from contextlib import ExitStack

import concourse.mybir as mybir
from concourse.masks import make_identity

F32 = mybir.dt.float32
BF16 = mybir.dt.bfloat16
I32 = mybir.dt.int32
U32 = mybir.dt.uint32
U8 = mybir.dt.uint8
FP8X4 = mybir.dt.float8_e4m3fn_x4
ALU = mybir.AluOpType
ACT = mybir.ActivationFunctionType

BATCH, TIME, JOINTS, CH = 8, 16, 32, 512
P = 128
PACK = 4
T_GROUPS = TIME * JOINTS // P
K_CHUNKS = CH // P
U_HALF = JOINTS // 2
PAIRS = U_HALF * JOINTS
HALVES = 2 * BATCH
PHI, THETA, KAPPA = 0, 1, 2

U_GPSIMD = 10

LEAD_TANH = 1
LEAD_SUBTRACT = 2
LEAD_MEANS = 4
LEAD_FIRST_PRODUCT = 5
LEAD_QUANTISE_X = 5
LEAD_TURN_X = 7

BANK_RING = 6

PLACE_BYTES = U_GPSIMD * JOINTS * PACK * 4

FLOPS = 2 * BATCH * TIME * JOINTS * CH * 2 * CH + 2 * BATCH * JOINTS * JOINTS * CH * CH


def tile_attgcn_pa_t_kernel(
    tc,
    x,
    A,
    lam,
    phi_w_words,
    phi_w_scales,
    phi_b,
    theta_w_words,
    theta_w_scales,
    theta_b,
    kappa_w_words,
    kappa_w_scales,
    kappa_b,
    out,
):
    nc = tc.nc
    with ExitStack() as ctx:
        ctx.enter_context(tc.manual_schedule())
        keep = ctx.enter_context(tc.tile_pool(name="keep", bufs=1))
        ring = ctx.enter_context(tc.tile_pool(name="ring", bufs=2))
        shared = ctx.enter_context(tc.tile_pool(name="shared", bufs=1))
        psum = ctx.enter_context(tc.psum_pool(name="psum", bufs=1))

        planes = keep.tile([P, 3, CH], U8, align_bytes=64)
        nc.vector.memset(planes[:].bitcast(I32), 0)

        def load_words(words_dram, name):
            words = keep.tile([P, CH], U32, align_bytes=64, name=name)
            nc.sync.dma_start(
                out=words[:].bitcast(I32),
                in_=words_dram[0].rearrange("p n t -> p (n t)").bitcast(I32),
            )
            return words

        def load_scales(scales_dram, which):
            for quadrant in range(4):
                nc.sync.dma_start(
                    out=planes[32 * quadrant : 32 * quadrant + 4, which, :].bitcast(I32),
                    in_=scales_dram[0, 4 * quadrant : 4 * quadrant + 4, :].bitcast(I32),
                )

        def load_x(b, pieces=1):
            by_group = x[b].rearrange("(g r) v c -> (r v) g c", g=T_GROUPS)
            x_rows = keep.tile([P, T_GROUPS, CH], BF16, name="x_rows%d" % b)
            groups = T_GROUPS // pieces
            for i in range(pieces):
                part = slice(i * groups, (i + 1) * groups)
                nc.sync.dma_start(out=x_rows[:, part, :], in_=by_group[:, part, :])
            return x_rows

        x_tiles = [load_x(0, 2)]
        load_scales(phi_w_scales, PHI)
        weight_words = [load_words(phi_w_words, "phi_words")]
        x_tiles.append(load_x(1))
        load_scales(theta_w_scales, THETA)
        weight_words.append(load_words(theta_w_words, "theta_words"))
        a_by_chunk = A.rearrange("(j k) u v -> j k (u v)", j=K_CHUNKS)
        a_bf = []
        for j in range(K_CHUNKS):
            a_chunk = keep.tile([P, JOINTS * JOINTS], BF16, name="a_bf%d" % j)
            nc.sync.dma_start(out=a_chunk[:], in_=a_by_chunk[j])
            a_bf.append(a_chunk)
        x_tiles.append(load_x(2))
        load_scales(kappa_w_scales, KAPPA)
        kappa_words = load_words(kappa_w_words, "kappa_words")
        for b in range(3, BATCH):
            x_tiles.append(load_x(b))

        ident = keep.tile([P, P], F32)
        make_identity(nc, ident[:])

        lam_bf = keep.tile([P, 1], BF16)
        nc.gpsimd.dma_start(out=lam_bf[:], in_=lam.partition_broadcast(P))
        kappa_b_bf = keep.tile([P, K_CHUNKS], BF16)
        with nc.allow_non_contiguous_dma(reason="512 bias values, one to a partition and chunk"):
            nc.gpsimd.dma_start(
                out=kappa_b_bf[:], in_=kappa_b.rearrange("(j k) -> k j", j=K_CHUNKS)
            )
        phi_b_bf = keep.tile([P, PACK], BF16)
        nc.gpsimd.dma_start(out=phi_b_bf[:], in_=phi_b.rearrange("(q k) -> q k", k=PACK))
        theta_b_bf = keep.tile([P, PACK], BF16)
        nc.gpsimd.dma_start(out=theta_b_bf[:], in_=theta_b.rearrange("(q k) -> q k", k=PACK))

        averager = keep.tile([P, JOINTS], F32)
        nc.vector.tensor_reduce(
            out=averager[:],
            in_=ident[:].rearrange("p (r v) -> p v r", v=JOINTS),
            axis=mybir.AxisListType.X,
            op=ALU.add,
        )
        nc.vector.tensor_scalar_mul(out=averager[:], in0=averager[:], scalar1=1.0 / TIME)

        warm = keep.tile([P, 1], F32)
        nc.vector.memset(warm[:], 0.0)
        nc.scalar.activation(out=warm[:], in_=warm[:], func=ACT.Tanh)

        lam_col = keep.tile([P, 1], F32)
        lam_kappa_b = keep.tile([P, K_CHUNKS], F32)
        bias_gap = keep.tile([P, PACK], F32)
        a_plus = []

        def prepare_small_vectors_and_a():
            nc.vector.tensor_copy(out=lam_col[:], in_=lam_bf[:])
            nc.vector.tensor_scalar_mul(
                out=lam_kappa_b[:], in0=kappa_b_bf[:], scalar1=lam_col[:, 0:1]
            )
            for j in range(K_CHUNKS):
                a_chunk = keep.tile([P, JOINTS * JOINTS], F32, name="a_plus%d" % j)
                nc.vector.tensor_scalar_add(
                    out=a_chunk[:], in0=a_bf[j][:], scalar1=lam_kappa_b[:, j : j + 1]
                )
                a_plus.append(a_chunk)
            nc.vector.tensor_tensor(
                out=bias_gap[:], in0=theta_b_bf[:], in1=phi_b_bf[:], op=ALU.subtract
            )

        grouped_x, x_codes, x_planes, partial_sums, mean_banks, th_shifted = {}, {}, {}, {}, {}, {}
        diffs_gpsimd, diffs_vector, f_rounded, f_codes, f_planes, mean_p_copies = {}, {}, {}, {}, {}, {}
        g_banks = {}

        def out_of_psum(engine, dst, src):
            if engine == "vector":
                nc.vector.tensor_copy(out=dst, in_=src)
            else:
                nc.scalar.copy(out=dst, in_=src)

        def turn_x(b, pair, engine="scalar"):
            if pair == 0:
                grouped = ring.tile([P, T_GROUPS * P, PACK], BF16, align_bytes=64, name="grouped")
                grouped_x[b] = grouped
            x_f32 = x_tiles[b][:].bitcast(F32)
            grouped_f32 = grouped_x[b][:].rearrange("q r k -> q (r k)").bitcast(F32)
            grouped_f32 = grouped_f32.rearrange("q (g r w) -> q g r w", g=T_GROUPS, w=2)
            turned = psum.tile([P, 2, 2, P], F32, tag="bank", bufs=BANK_RING)
            for g in range(2):
                for w in range(2):
                    nc.tensor.transpose(
                        turned[:, g, w, :], x_f32[:, 2 * pair + g, w : CH // 2 : 2], ident[:]
                    )
            out_of_psum(
                engine,
                grouped_f32[:, 2 * pair : 2 * pair + 2, :, :],
                turned[:].rearrange("q g w r -> q g r w"),
            )

        def quantise_x(b):
            codes = keep.tile([P, T_GROUPS * P], U32, align_bytes=64, name="x_codes%d" % b)
            plane = keep.tile([P, T_GROUPS * P], U8, align_bytes=64, name="x_plane%d" % b)
            nc.vector.quantize_mx(
                out=codes[:].bitcast(FP8X4),
                scales=plane[:],
                in_=grouped_x[b][:].rearrange("q r k -> q (r k)"),
            )
            x_codes[b], x_planes[b] = codes, plane

        def first_product(half, engine="scalar"):
            b, which = half // 2, half % 2
            acc = psum.tile([P, CH], F32, tag="bank", bufs=BANK_RING)
            for g in range(T_GROUPS):
                rows = slice(g * P, (g + 1) * P)
                nc.tensor.matmul_mx(
                    out=acc[:],
                    lhsT=x_codes[b][:, rows].bitcast(FP8X4),
                    lhsT_scale=x_planes[b][:, rows],
                    rhs=weight_words[which][:].bitcast(FP8X4),
                    rhs_scale=planes[:, which, :],
                    start=(g == 0),
                    stop=(g == T_GROUPS - 1),
                )
            partial = ring.tile([P, PACK, P], F32, name="partial")
            out_of_psum(engine, partial[:], acc[:].rearrange("r (q k) -> r k q", k=PACK))
            partial_sums[half] = partial

        def means(half):
            b, which = half // 2, half % 2
            if which == PHI:
                mean_bank = psum.tile([P, 2, PACK, JOINTS], F32, bufs=2, name="mean_bank")
                mean_banks[b] = mean_bank
            for k in range(PACK):
                nc.tensor.matmul(
                    out=mean_banks[b][:, which, k, :],
                    lhsT=partial_sums[half][:, k, :],
                    rhs=averager[:],
                    start=True,
                    stop=True,
                )

        def shift_mean_th(b):
            shifted = ring.tile([P, JOINTS, PACK], F32, name="shifted")
            nc.vector.tensor_tensor(
                out=shifted[:],
                in0=mean_banks[b][:, THETA, :, :].rearrange("q k v -> q v k"),
                in1=bias_gap[:].unsqueeze(1).to_broadcast([P, JOINTS, PACK]),
                op=ALU.add,
            )
            th_shifted[b] = shifted

        def copy_mean_p(b):
            p_copy = ring.tile([P, JOINTS, PACK], F32, name="p_copy")
            nc.scalar.copy(out=p_copy[:], in_=mean_banks[b][:, PHI, :, :].rearrange("q k u -> q u k"))
            mean_p_copies[b] = p_copy

        def mean_p_of(half, first, last):
            u0 = (half % 2) * U_HALF
            bank = mean_banks[half // 2]
            return bank[:, PHI, :, u0 + first : u0 + last].rearrange("q k u -> q u k")

        def gpsimd_share(half):
            return U_GPSIMD if half >= 2 else 0

        def place(half):
            return (half % 3) * PLACE_BYTES

        def subtract_on_gpsimd(half):
            share = gpsimd_share(half)
            if share > 0:
                diff = shared.tile(
                    [P, share, JOINTS, PACK], F32, offset=place(half), align_bytes=64,
                    name="diff_gpsimd%d" % (half % 3),
                )
                diffs_gpsimd[half] = diff
                u0 = (half % 2) * U_HALF
                shape = [P, share, JOINTS, PACK]
                nc.gpsimd.tensor_tensor(
                    out=diff[:],
                    in0=mean_p_copies[half // 2][:, u0 : u0 + share, :].unsqueeze(2).to_broadcast(shape),
                    in1=th_shifted[half // 2][:].unsqueeze(1).to_broadcast(shape),
                    op=ALU.subtract,
                )

        def subtract_on_vector(half):
            share = gpsimd_share(half)
            shape = [P, U_HALF - share, JOINTS, PACK]
            diff = ring.tile(shape, F32, bufs=3, name="diff_vector")
            diffs_vector[half] = diff
            nc.vector.tensor_tensor(
                out=diff[:],
                in0=mean_p_of(half, share, U_HALF).unsqueeze(2).to_broadcast(shape),
                in1=th_shifted[half // 2][:].unsqueeze(1).to_broadcast(shape),
                op=ALU.subtract,
            )

        def tanh(half):
            share = gpsimd_share(half)
            rounded = shared.tile(
                [P, PAIRS * PACK], BF16, offset=place(half + 2), align_bytes=64,
                name="rounded%d" % (half % 3),
            )
            split = share * JOINTS * PACK
            if share > 0:
                nc.scalar.activation(
                    out=rounded[:, 0:split],
                    in_=diffs_gpsimd[half][:].rearrange("q u v k -> q (u v k)"),
                    func=ACT.Tanh,
                )
            nc.scalar.activation(
                out=rounded[:, split : PAIRS * PACK],
                in_=diffs_vector[half][:].rearrange("q u v k -> q (u v k)"),
                func=ACT.Tanh,
            )
            f_rounded[half] = rounded

        def quantise_f(half):
            codes = ring.tile([P, PAIRS], U32, align_bytes=64, bufs=3, name="f_codes")
            plane = ring.tile([P, PAIRS], U8, align_bytes=64, bufs=3, name="f_plane")
            nc.vector.quantize_mx(
                out=codes[:].bitcast(FP8X4), scales=plane[:], in_=f_rounded[half][:]
            )
            f_codes[half], f_planes[half] = codes, plane

        def second_product(half, pair):
            for j in (2 * pair, 2 * pair + 1):
                cols = slice(j * P, (j + 1) * P)
                g_ps = psum.tile([P, PAIRS], F32, tag="bank", bufs=BANK_RING)
                nc.tensor.matmul_mx(
                    out=g_ps[:],
                    lhsT=kappa_words[:, cols].bitcast(FP8X4),
                    lhsT_scale=planes[:, KAPPA, cols],
                    rhs=f_codes[half][:].bitcast(FP8X4),
                    rhs_scale=f_planes[half][:],
                    start=True,
                    stop=True,
                )
                g_banks[(half, j)] = g_ps

        def finish_and_store(half, pair):
            pairs = slice((half % 2) * PAIRS, (half % 2 + 1) * PAIRS)
            out_b = out[half // 2].rearrange("(j k) u v -> k j (u v)", j=K_CHUNKS)
            result = ring.tile([P, 2, PAIRS], F32, bufs=6, name="result")
            for i in range(2):
                j = 2 * pair + i
                nc.vector.scalar_tensor_tensor(
                    out=result[:, i, :],
                    in0=g_banks[(half, j)][:],
                    scalar=lam_col[:, 0:1],
                    in1=a_plus[j][:, pairs],
                    op0=ALU.mult,
                    op1=ALU.add,
                )
            nc.sync.dma_start(out=out_b[:, 2 * pair : 2 * pair + 2, pairs], in_=result[:])

        turn_x(0, 0)
        turn_x(0, 1, "vector")
        quantise_x(0)
        turn_x(1, 0)
        turn_x(1, 1)
        first_product(0)
        first_product(1)
        quantise_x(1)
        prepare_small_vectors_and_a()
        means(0)
        means(1)
        shift_mean_th(0)
        turn_x(2, 0)
        turn_x(2, 1)
        first_product(2)
        subtract_on_gpsimd(0)
        subtract_on_vector(0)
        tanh(0)
        quantise_x(2)
        first_product(3, "vector")
        subtract_on_gpsimd(1)
        subtract_on_vector(1)
        means(2)
        means(3)
        shift_mean_th(1)
        copy_mean_p(1)
        first_product(4)
        turn_x(3, 0)

        def step(s):
            if s + LEAD_TURN_X < HALVES:
                turn_x((s + LEAD_TURN_X) // 2, (s + LEAD_TURN_X) % 2)
            if (s + LEAD_QUANTISE_X) % 2 == 0 and (s + LEAD_QUANTISE_X) // 2 < BATCH:
                quantise_x((s + LEAD_QUANTISE_X) // 2)
            quantise_f(s)
            if s + LEAD_SUBTRACT < HALVES:
                subtract_on_gpsimd(s + LEAD_SUBTRACT)
            second_product(s, 0)
            if s + LEAD_SUBTRACT < HALVES:
                subtract_on_vector(s + LEAD_SUBTRACT)
            if s + LEAD_TANH < HALVES:
                tanh(s + LEAD_TANH)
            if s > 0:
                finish_and_store(s - 1, 1)
            if s + LEAD_MEANS < HALVES:
                means(s + LEAD_MEANS)
                if (s + LEAD_MEANS) % 2 == THETA:
                    copy_mean_p((s + LEAD_MEANS) // 2)
            if s + LEAD_FIRST_PRODUCT < HALVES:
                first_product(s + LEAD_FIRST_PRODUCT)
            second_product(s, 1)
            finish_and_store(s, 0)
            if s + LEAD_MEANS < HALVES and (s + LEAD_MEANS) % 2 == THETA:
                shift_mean_th((s + LEAD_MEANS) // 2)

        for s in range(HALVES):
            step(s)
        finish_and_store(HALVES - 1, 1)
